import numpy as np
import ml_dtypes


def mxq(x, axis, fmt="e4m3"):
    dtype, down = {"e4m3": (ml_dtypes.float8_e4m3fn, 7), "e5m2": (ml_dtypes.float8_e5m2, 14)}[fmt]
    v = np.moveaxis(np.asarray(x, np.float32).astype(ml_dtypes.bfloat16).astype(np.float64), axis, -1)
    blocks = v.reshape(v.shape[:-1] + (-1, 32))
    amax = np.abs(blocks).max(-1, keepdims=True)
    byte = np.maximum(np.where(amax > 0, np.frexp(amax)[1] - 1 + 127, 0) - down, 1)
    scale = np.exp2(byte - 127.0)
    codes = (blocks / scale).astype(np.float32).astype(dtype).astype(np.float64)
    return np.moveaxis((codes * scale).reshape(v.shape), -1, axis)


WIDE = False


def mx_kscale(k):
    if not WIDE:
        return np.ones(k)
    levels = np.array([10, -10, 5, -5, 0])
    a = np.random.permutation(np.resize(levels, k // 512 * 4)).reshape(k // 512, 4)
    idx = np.arange(k)
    return np.exp2(a[idx // 512, idx % 128 // 32])


BF16 = ml_dtypes.bfloat16


def bf(x):
    return np.asarray(x, np.float32).astype(BF16)


def f64(x):
    return np.asarray(x).astype(np.float64)


B, HH, WW, C, NH, KD, WS, SS = 2, 64, 64, 512, 2, 64, 8, 4
GH, GW, T, F = HH // WS, WW // WS, WS * WS, NH * KD
N = B * GH * GW


def setup_inputs():
    s = mx_kscale(C)

    def weight():
        return bf(np.random.standard_normal((C, NH, KD)) / np.sqrt(C) / s[:, None, None])

    def bias():
        return bf(np.random.standard_normal((NH, KD)) * 0.3)

    return {"x": bf(np.random.standard_normal((B, HH, WW, C)) * s), "wq": weight(), "bq": bias(),
            "wk": weight(), "bk": bias(), "wv": weight(), "bv": bias()}


def reference(x, wq, bq, wk, bk, wv, bv):
    shifted = np.roll(f64(x), shift=(-SS, -SS), axis=(1, 2))
    win = shifted.reshape(B, GH, WS, GW, WS, C).swapaxes(2, 3).reshape(N * T, C)
    wn = mxq(win, 1, "e4m3")
    q = (wn @ mxq(f64(wq).reshape(C, F), 0, "e4m3")).reshape(N, T, NH, KD) + f64(bq)
    k = (wn @ mxq(f64(wk).reshape(C, F), 0, "e4m3")).reshape(N, T, NH, KD) + f64(bk)
    v = (wn @ mxq(f64(wv).reshape(C, F), 0, "e4m3")).reshape(N, T, NH, KD) + f64(bv)
    return q, k, v

@@ -1,0 +1,179 @@
+from contextlib import ExitStack
+
+import concourse.mybir as mybir
+from concourse.masks import make_identity
+
+FP8X4 = mybir.dt.float8_e4m3fn_x4
+BF16 = mybir.dt.bfloat16
+F32 = mybir.dt.float32
+U32 = mybir.dt.uint32
+U8 = mybir.dt.uint8
+
+P = 128
+FLOPS = 2 * 8192 * 512 * 384
+MANUAL = True
+SLABS = (0, 1, 3, 2, 7, 4, 5, 6)
+
+
+def tile_windowattentionblock_pa_t_kernel(tc, x, wq, bq, wk, bk, wv, bv, out_0, out_1, out_2):
+    nc = tc.nc
+    weights = (wq, wk, wv)
+    biases = (bq, bk, bv)
+    outs = [o.rearrange("n (ti tj) h d -> (n ti) (tj h d)", tj=8) for o in (out_0, out_1, out_2)]
+    xc = x.rearrange("b i (aj rj) c -> (b i aj) (rj c)", rj=8)
+
+    with ExitStack() as ctx:
+        const = ctx.enter_context(tc.tile_pool(name="const", bufs=1))
+        xpool = ctx.enter_context(tc.tile_pool(name="xpool", bufs=1))
+        gpool = ctx.enter_context(tc.tile_pool(name="gpool", bufs=3))
+        qpool = ctx.enter_context(tc.tile_pool(name="qpool", bufs=3))
+        opool = ctx.enter_context(tc.tile_pool(name="opool", bufs=6))
+        psum_t = ctx.enter_context(tc.psum_pool(name="psum_t", bufs=4))
+        psum_o = ctx.enter_context(tc.psum_pool(name="psum_o", bufs=4))
+        if MANUAL:
+            ctx.enter_context(tc.manual_schedule())
+
+        b_row = const.tile([P, 512], BF16, name="b_row")
+        nc.vector.memset(b_row[:], 0.0)
+        ones = const.tile([P, P], BF16, name="ones")
+        nc.vector.memset(ones[:], 1.0)
+
+        w_raw = const.tile([P, 3, 4, P], BF16, name="w_raw")
+        for m in range(3):
+            nc.scalar.dma_start(
+                out=w_raw[:, m, :, :].rearrange("p (u e) f -> p u (e f)", u=2),
+                in_=weights[m].rearrange("(u p e) h d -> p u (e h d)", u=2, e=2),
+            )
+        x_sb = {}
+        for pos, k in enumerate(SLABS):
+            x_t = xpool.tile([P, 4096], BF16, name="x%d" % k)
+            x_sb[k] = x_t
+            b, a = divmod(k, 4)
+            c0 = (b * 64 + 16 * a + 4) * 8
+            if pos == 0:
+                nc.sync.dma_start(out=x_t[:, 2048:4096], in_=xc[c0:c0 + P, 2048:4096])
+                nc.sync.dma_start(out=x_t[:, 0:2048], in_=xc[c0:c0 + P, 0:2048])
+                for m in range(3):
+                    nc.sync.dma_start(
+                        out=b_row[0:1, m * P:(m + 1) * P],
+                        in_=biases[m].rearrange("(o h) d -> o (h d)", o=1),
+                    )
+            elif a < 3:
+                nc.sync.dma_start(out=x_t[:], in_=xc[c0:c0 + P, :])
+            else:
+                nc.sync.dma_start(out=x_t[0:96, :], in_=xc[c0:c0 + 96, :])
+                nc.sync.dma_start(out=x_t[96:P, :], in_=xc[b * 512:b * 512 + 32, :])
+
+
+        ident = const.tile([P, P], F32, name="ident")
+        make_identity(nc, ident[:])
+        pa = const.tile([P, P], F32, name="pa")
+        pb = const.tile([P, P], F32, name="pb")
+        src = ident[:].rearrange("p (g t a) -> p g a t", g=2, t=8)
+        pav = pa[:].rearrange("p (g a t) -> p g a t", g=2, a=8)
+        pbv = pb[:].rearrange("p (g a t) -> p g a t", g=2, a=8)
+        nc.gpsimd.tensor_copy(out=pav, in_=src)
+        nc.gpsimd.tensor_copy(out=pbv[:, :, 0:7, :], in_=src[:, :, 1:8, :])
+        nc.gpsimd.tensor_copy(out=pbv[:, :, 7:8, :], in_=src[:, :, 0:1, :])
+
+        w_grp = const.tile([P, 3, P, 4], BF16, name="w_grp", align_bytes=64)
+        w_codes = const.tile([P, 384], U32, name="w_codes", align_bytes=64)
+        w_scales = const.tile([P, 384], U8, name="w_scales", align_bytes=64)
+        for m in range(3):
+            nc.vector.tensor_copy(out=w_grp[:, m, :, :], in_=w_raw[:, m, :, :].rearrange("p t f -> p f t"))
+        nc.vector.quantize_mx(
+            out=w_codes[:, 0:256].bitcast(FP8X4),
+            scales=w_scales[:, 0:256],
+            in_=w_grp[:, 0:2, :, :].rearrange("p m f t -> p (m f t)"),
+        )
+        nc.vector.quantize_mx(
+            out=w_codes[:, 256:384].bitcast(FP8X4),
+            scales=w_scales[:, 256:384],
+            in_=w_grp[:, 2, :, :].rearrange("p f t -> p (f t)"),
+        )
+
+        bias_sb = const.tile([P, 3, P], F32, name="bias_sb")
+
+        def spread_bias():
+            bias_ps = psum_o.tile([P, 512], F32, name="acc")
+            nc.tensor.matmul(out=bias_ps[:], lhsT=ones[:], rhs=b_row[:], start=True, stop=True)
+            nc.scalar.copy(out=bias_sb[:].rearrange("p m f -> p (m f)"), in_=bias_ps[:, 0:384])
+
+        units = [(k, hb) for k in SLABS for hb in range(2)]
+        state = {}
+
+        def transposes(h):
+            ti, hb = units[h]
+            perm = pa if hb == 0 else pb
+            xf = x_sb[ti][:].bitcast(F32)
+            g = gpool.tile([P, 2048], BF16, name="g", align_bytes=64)
+            gf = g[:].bitcast(F32).rearrange("p (a r u) -> p a r u", a=4, u=2)
+            for a2 in range(2):
+                xt = psum_t.tile([P, 2, 2, P], F32, name="xt")
+                for a in range(2):
+                    rj = (4 * hb + 2 * a2 + a + 4) % 8
+                    for u in range(2):
+                        c0 = rj * 256 + u * P
+                        nc.tensor.transpose(xt[:, a, u, :], xf[:, c0:c0 + P], perm[:])
+                nc.scalar.copy(out=gf[:, 2 * a2:2 * a2 + 2, :, :], in_=xt[:].rearrange("p a u r -> p a r u"))
+            state[("g", h)] = g
+
+        def quantise(h):
+            g = state[("g", h)]
+            codes = qpool.tile([P, 512], U32, name="codes", align_bytes=64)
+            scales = qpool.tile([P, 512], U8, name="scales", align_bytes=64)
+            nc.vector.quantize_mx(out=codes[:].bitcast(FP8X4), scales=scales[:], in_=g[:])
+            state[("q", h)] = (codes, scales)
+
+        def project(h, a):
+            ti, hb = units[h]
+            codes, scales = state[("q", h)]
+            if hb == 0 and a == 0:
+                state[("o", ti)] = opool.tile([P, 3, 8, P], F32, name="o_sb")
+            o_sb = state[("o", ti)]
+            acc = psum_o.tile([P, 512], F32, name="acc")
+            cols = slice(a * P, (a + 1) * P)
+            for n0, n1 in ((0, 256), (256, 384)):
+                nc.tensor.matmul_mx(
+                    out=acc[:, n0:n1],
+                    lhsT=codes[:, cols].bitcast(FP8X4),
+                    lhsT_scale=scales[:, cols],
+                    rhs=w_codes[:, n0:n1].bitcast(FP8X4),
+                    rhs_scale=w_scales[:, n0:n1],
+                    start=True,
+                    stop=True,
+                )
+            nc.vector.tensor_tensor(
+                out=o_sb[:, :, 4 * hb + a, :],
+                in0=acc[:, 0:384].rearrange("p (m f) -> p m f", m=3),
+                in1=bias_sb[:],
+                op=mybir.AluOpType.add,
+            )
+
+        def store(ti, t0, t1):
+            o_sb = state[("o", ti)]
+            for m in range(3):
+                nc.sync.dma_start(
+                    out=outs[m][ti * P:(ti + 1) * P, t0 * P:t1 * P],
+                    in_=o_sb[:, m, t0:t1, :].rearrange("p t f -> p (t f)"),
+                )
+
+        n_units = len(units)
+        transposes(0)
+        quantise(0)
+        for h in range(n_units):
+            ti, hb = units[h]
+            if h + 1 < n_units:
+                transposes(h + 1)
+            if h == 0:
+                spread_bias()
+            project(h, 0)
+            project(h, 1)
+            if h + 1 < n_units:
+                quantise(h + 1)
+            project(h, 2)
+            project(h, 3)
+            if h >= n_units - 2:
+                store(ti, 4 * hb, 4 * hb + 4)
+            elif hb == 1:
+                store(ti, 0, 8)

@@ -27,9 +27,9 @@ def tile_windowattentionblock_pa_t_kernel(tc, x, wq, bq, wk, bk, wv, bv, out_0, 
         xpool = ctx.enter_context(tc.tile_pool(name="xpool", bufs=1))
         gpool = ctx.enter_context(tc.tile_pool(name="gpool", bufs=3))
         qpool = ctx.enter_context(tc.tile_pool(name="qpool", bufs=3))
-        opool = ctx.enter_context(tc.tile_pool(name="opool", bufs=6))
-        psum_t = ctx.enter_context(tc.psum_pool(name="psum_t", bufs=4))
-        psum_o = ctx.enter_context(tc.psum_pool(name="psum_o", bufs=4))
+        opool = ctx.enter_context(tc.tile_pool(name="opool", bufs=8))
+        psum_t = ctx.enter_context(tc.psum_pool(name="psum_t", bufs=2))
+        psum_o = ctx.enter_context(tc.psum_pool(name="psum_o", bufs=6))
         if MANUAL:
             ctx.enter_context(tc.manual_schedule())
 
@@ -125,30 +125,48 @@ def tile_windowattentionblock_pa_t_kernel(tc, x, wq, bq, wk, bk, wv, bv, out_0, 
             nc.vector.quantize_mx(out=codes[:].bitcast(FP8X4), scales=scales[:], in_=g[:])
             state[("q", h)] = (codes, scales)
 
-        def project(h, a):
+        def mx(out, codes, scales, a, n0, n1):
+            cols = slice(a * P, (a + 1) * P)
+            nc.tensor.matmul_mx(
+                out=out,
+                lhsT=codes[:, cols].bitcast(FP8X4),
+                lhsT_scale=scales[:, cols],
+                rhs=w_codes[:, n0:n1].bitcast(FP8X4),
+                rhs_scale=w_scales[:, n0:n1],
+                start=True,
+                stop=True,
+            )
+
+        def project(h, half):
             ti, hb = units[h]
             codes, scales = state[("q", h)]
-            if hb == 0 and a == 0:
+            if hb == 0 and half == 0:
                 state[("o", ti)] = opool.tile([P, 3, 8, P], F32, name="o_sb")
             o_sb = state[("o", ti)]
-            acc = psum_o.tile([P, 512], F32, name="acc")
-            cols = slice(a * P, (a + 1) * P)
-            for n0, n1 in ((0, 256), (256, 384)):
-                nc.tensor.matmul_mx(
-                    out=acc[:, n0:n1],
-                    lhsT=codes[:, cols].bitcast(FP8X4),
-                    lhsT_scale=scales[:, cols],
-                    rhs=w_codes[:, n0:n1].bitcast(FP8X4),
-                    rhs_scale=w_scales[:, n0:n1],
-                    start=True,
-                    stop=True,
-                )
+            if half == 0:
+                state[("z", h)] = psum_o.tile([P, 4, P], F32, name="acc")
+            zb = state[("z", h)]
+            qk = psum_o.tile([P, 2, 2, P], F32, name="acc")
+            for i in range(2):
+                a = 2 * half + i
+                mx(qk[:, i, :, :].rearrange("p m f -> p (m f)"), codes, scales, a, 0, 256)
+                mx(zb[:, a, :], codes, scales, a, 256, 384)
+            t0 = 4 * hb + 2 * half
             nc.vector.tensor_tensor(
-                out=o_sb[:, :, 4 * hb + a, :],
-                in0=acc[:, 0:384].rearrange("p (m f) -> p m f", m=3),
-                in1=bias_sb[:],
+                out=o_sb[:, 0:2, t0:t0 + 2, :],
+                in0=qk[:].rearrange("p t m f -> p m t f"),
+                in1=bias_sb[:, 0:2, :].unsqueeze(2).to_broadcast([P, 2, 2, P]),
                 op=mybir.AluOpType.add,
             )
+            if half == 1:
+                v_sb = o_sb[:, 2, 4 * hb:4 * hb + 4, :]
+                nc.scalar.copy(out=v_sb, in_=zb[:])
+                nc.gpsimd.tensor_tensor(
+                    out=v_sb,
+                    in0=v_sb,
+                    in1=bias_sb[:, 2:3, :].to_broadcast([P, 4, P]),
+                    op=mybir.AluOpType.add,
+                )
 
         def store(ti, t0, t1):
             o_sb = state[("o", ti)]
@@ -168,11 +186,9 @@ def tile_windowattentionblock_pa_t_kernel(tc, x, wq, bq, wk, bk, wv, bv, out_0, 
             if h == 0:
                 spread_bias()
             project(h, 0)
-            project(h, 1)
             if h + 1 < n_units:
                 quantise(h + 1)
-            project(h, 2)
-            project(h, 3)
+            project(h, 1)
             if h >= n_units - 2:
                 store(ti, 4 * hb, 4 * hb + 4)
             elif hb == 1:

@@ -12,6 +12,8 @@ U8 = mybir.dt.uint8
 P = 128
 FLOPS = 2 * 8192 * 512 * 384
 MANUAL = True
+LOOK_T = 3
+LOOK_Q = 2
 SLABS = (0, 1, 3, 2, 7, 4, 5, 6)
 
 
@@ -26,7 +28,7 @@ def tile_windowattentionblock_pa_t_kernel(tc, x, wq, bq, wk, bk, wv, bv, out_0, 
         const = ctx.enter_context(tc.tile_pool(name="const", bufs=1))
         xpool = ctx.enter_context(tc.tile_pool(name="xpool", bufs=1))
         gpool = ctx.enter_context(tc.tile_pool(name="gpool", bufs=3))
-        qpool = ctx.enter_context(tc.tile_pool(name="qpool", bufs=3))
+        qpool = ctx.enter_context(tc.tile_pool(name="qpool", bufs=4))
         opool = ctx.enter_context(tc.tile_pool(name="opool", bufs=8))
         psum_t = ctx.enter_context(tc.psum_pool(name="psum_t", bufs=2))
         psum_o = ctx.enter_context(tc.psum_pool(name="psum_o", bufs=6))
@@ -177,17 +179,27 @@ def tile_windowattentionblock_pa_t_kernel(tc, x, wq, bq, wk, bk, wv, bv, out_0, 
                 )
 
         n_units = len(units)
-        transposes(0)
-        quantise(0)
+        done = {"t": 0, "q": 0}
+
+        def transposes_upto(last):
+            while done["t"] <= min(last, n_units - 1):
+                transposes(done["t"])
+                done["t"] += 1
+
+        def quantise_upto(last):
+            while done["q"] <= min(last, n_units - 1):
+                quantise(done["q"])
+                done["q"] += 1
+
+        transposes_upto(0)
+        quantise_upto(0)
         for h in range(n_units):
             ti, hb = units[h]
-            if h + 1 < n_units:
-                transposes(h + 1)
+            transposes_upto(h + min(LOOK_T, h + 1))
             if h == 0:
                 spread_bias()
             project(h, 0)
-            if h + 1 < n_units:
-                quantise(h + 1)
+            quantise_upto(h + min(LOOK_Q, h + 1))
             project(h, 1)
             if h >= n_units - 2:
                 store(ti, 4 * hb, 4 * hb + 4)

@@ -63,8 +63,9 @@ def tile_windowattentionblock_pa_t_kernel(tc, x, wq, bq, wk, bk, wv, bv, out_0, 
             elif a < 3:
                 nc.sync.dma_start(out=x_t[:], in_=xc[c0:c0 + P, :])
             else:
-                nc.sync.dma_start(out=x_t[0:96, :], in_=xc[c0:c0 + 96, :])
-                nc.sync.dma_start(out=x_t[96:P, :], in_=xc[b * 512:b * 512 + 32, :])
+                for s in range(4):
+                    cs = c0 + 32 * s if s < 3 else b * 512
+                    nc.sync.dma_start(out=x_t[s:P:4, :], in_=xc[cs:cs + 32, :])
 
 
         ident = const.tile([P, P], F32, name="ident")
@@ -77,6 +78,15 @@ def tile_windowattentionblock_pa_t_kernel(tc, x, wq, bq, wk, bk, wv, bv, out_0, 
         nc.gpsimd.tensor_copy(out=pav, in_=src)
         nc.gpsimd.tensor_copy(out=pbv[:, :, 0:7, :], in_=src[:, :, 1:8, :])
         nc.gpsimd.tensor_copy(out=pbv[:, :, 7:8, :], in_=src[:, :, 0:1, :])
+        paw = const.tile([P, P], F32, name="paw")
+        pbw = const.tile([P, P], F32, name="pbw")
+        srcw = ident[:].rearrange("p (tl a g th) -> p g a th tl", tl=4, a=8, g=2)
+        pawv = paw[:].rearrange("p (g a th tl) -> p g a th tl", g=2, a=8, th=2)
+        pbwv = pbw[:].rearrange("p (g a th tl) -> p g a th tl", g=2, a=8, th=2)
+        for gg in range(2):
+            nc.vector.tensor_copy(out=pawv[:, gg, :, :, :], in_=srcw[:, gg, :, :, :])
+            nc.vector.tensor_copy(out=pbwv[:, gg, 0:7, :, :], in_=srcw[:, gg, 1:8, :, :])
+            nc.vector.tensor_copy(out=pbwv[:, gg, 7:8, :, :], in_=srcw[:, gg, 0:1, :, :])
 
         w_grp = const.tile([P, 3, P, 4], BF16, name="w_grp", align_bytes=64)
         w_codes = const.tile([P, 384], U32, name="w_codes", align_bytes=64)
@@ -106,7 +116,10 @@ def tile_windowattentionblock_pa_t_kernel(tc, x, wq, bq, wk, bk, wv, bv, out_0, 
 
         def transposes(h):
             ti, hb = units[h]
-            perm = pa if hb == 0 else pb
+            if ti % 4 == 3:
+                perm = paw if hb == 0 else pbw
+            else:
+                perm = pa if hb == 0 else pb
             xf = x_sb[ti][:].bitcast(F32)
             g = gpool.tile([P, 2048], BF16, name="g", align_bytes=64)
             gf = g[:].bitcast(F32).rearrange("p (a r u) -> p a r u", a=4, u=2)

@@ -8,32 +8,31 @@ BF16 = mybir.dt.bfloat16
 F32 = mybir.dt.float32
 U32 = mybir.dt.uint32
 U8 = mybir.dt.uint8
+ADD = mybir.AluOpType.add
 
 P = 128
 FLOPS = 2 * 8192 * 512 * 384
-MANUAL = True
-LOOK_T = 3
-LOOK_Q = 2
-SLABS = (0, 1, 3, 2, 7, 4, 5, 6)
+N_GROUPS = 4
+N_UNITS = 16
+N_JOBS = 48
 
 
 def tile_windowattentionblock_pa_t_kernel(tc, x, wq, bq, wk, bk, wv, bv, out_0, out_1, out_2):
     nc = tc.nc
     weights = (wq, wk, wv)
     biases = (bq, bk, bv)
-    outs = [o.rearrange("n (ti tj) h d -> (n ti) (tj h d)", tj=8) for o in (out_0, out_1, out_2)]
+    outs = [o.rearrange("n (tp r) h d -> (n tp) (r h d)", r=16) for o in (out_0, out_1, out_2)]
     xc = x.rearrange("b i (aj rj) c -> (b i aj) (rj c)", rj=8)
 
     with ExitStack() as ctx:
         const = ctx.enter_context(tc.tile_pool(name="const", bufs=1))
         xpool = ctx.enter_context(tc.tile_pool(name="xpool", bufs=1))
         gpool = ctx.enter_context(tc.tile_pool(name="gpool", bufs=3))
-        qpool = ctx.enter_context(tc.tile_pool(name="qpool", bufs=4))
-        opool = ctx.enter_context(tc.tile_pool(name="opool", bufs=8))
+        qpool = ctx.enter_context(tc.tile_pool(name="qpool", bufs=8))
+        opool = ctx.enter_context(tc.tile_pool(name="opool", bufs=12))
         psum_t = ctx.enter_context(tc.psum_pool(name="psum_t", bufs=2))
         psum_o = ctx.enter_context(tc.psum_pool(name="psum_o", bufs=6))
-        if MANUAL:
-            ctx.enter_context(tc.manual_schedule())
+        ctx.enter_context(tc.manual_schedule())
 
         b_row = const.tile([P, 512], BF16, name="b_row")
         nc.vector.memset(b_row[:], 0.0)
@@ -46,47 +45,55 @@ def tile_windowattentionblock_pa_t_kernel(tc, x, wq, bq, wk, bk, wv, bv, out_0, 
                 out=w_raw[:, m, :, :].rearrange("p (u e) f -> p u (e f)", u=2),
                 in_=weights[m].rearrange("(u p e) h d -> p u (e h d)", u=2, e=2),
             )
-        x_sb = {}
-        for pos, k in enumerate(SLABS):
-            x_t = xpool.tile([P, 4096], BF16, name="x%d" % k)
-            x_sb[k] = x_t
+        x_sb = [xpool.tile([P, 4096], BF16, name="x%d" % k) for k in range(8)]
+
+        def first_chunk(k):
             b, a = divmod(k, 4)
-            c0 = (b * 64 + 16 * a + 4) * 8
-            if pos == 0:
-                nc.sync.dma_start(out=x_t[:, 2048:4096], in_=xc[c0:c0 + P, 2048:4096])
-                nc.sync.dma_start(out=x_t[:, 0:2048], in_=xc[c0:c0 + P, 0:2048])
-                for m in range(3):
-                    nc.sync.dma_start(
-                        out=b_row[0:1, m * P:(m + 1) * P],
-                        in_=biases[m].rearrange("(o h) d -> o (h d)", o=1),
-                    )
-            elif a < 3:
-                nc.sync.dma_start(out=x_t[:], in_=xc[c0:c0 + P, :])
+            return (b * 64 + 16 * a + 4) * 8
+
+        for lo in (2048, 0):
+            for k in range(2):
+                c0 = first_chunk(k)
+                nc.sync.dma_start(out=x_sb[k][:, lo:lo + 2048], in_=xc[c0:c0 + P, lo:lo + 2048])
+        for m in range(3):
+            nc.sync.dma_start(
+                out=b_row[0:1, m * P:(m + 1) * P],
+                in_=biases[m].rearrange("(o h) d -> o (h d)", o=1),
+            )
+        for k in range(2, 8):
+            c0 = first_chunk(k)
+            if k % 4 < 3:
+                nc.sync.dma_start(out=x_sb[k][:], in_=xc[c0:c0 + P, :])
             else:
                 for s in range(4):
-                    cs = c0 + 32 * s if s < 3 else b * 512
-                    nc.sync.dma_start(out=x_t[s:P:4, :], in_=xc[cs:cs + 32, :])
-
+                    cs = c0 + 32 * s if s < 3 else (k // 4) * 512
+                    nc.sync.dma_start(out=x_sb[k][s:P:4, :], in_=xc[cs:cs + 32, :])
 
         ident = const.tile([P, P], F32, name="ident")
         make_identity(nc, ident[:])
-        pa = const.tile([P, P], F32, name="pa")
-        pb = const.tile([P, P], F32, name="pb")
-        src = ident[:].rearrange("p (g t a) -> p g a t", g=2, t=8)
-        pav = pa[:].rearrange("p (g a t) -> p g a t", g=2, a=8)
-        pbv = pb[:].rearrange("p (g a t) -> p g a t", g=2, a=8)
-        nc.gpsimd.tensor_copy(out=pav, in_=src)
-        nc.gpsimd.tensor_copy(out=pbv[:, :, 0:7, :], in_=src[:, :, 1:8, :])
-        nc.gpsimd.tensor_copy(out=pbv[:, :, 7:8, :], in_=src[:, :, 0:1, :])
-        paw = const.tile([P, P], F32, name="paw")
-        pbw = const.tile([P, P], F32, name="pbw")
-        srcw = ident[:].rearrange("p (tl a g th) -> p g a th tl", tl=4, a=8, g=2)
-        pawv = paw[:].rearrange("p (g a th tl) -> p g a th tl", g=2, a=8, th=2)
-        pbwv = pbw[:].rearrange("p (g a th tl) -> p g a th tl", g=2, a=8, th=2)
-        for gg in range(2):
-            nc.vector.tensor_copy(out=pawv[:, gg, :, :, :], in_=srcw[:, gg, :, :, :])
-            nc.vector.tensor_copy(out=pbwv[:, gg, 0:7, :, :], in_=srcw[:, gg, 1:8, :, :])
-            nc.vector.tensor_copy(out=pbwv[:, gg, 7:8, :, :], in_=srcw[:, gg, 0:1, :, :])
+        perm = {}
+        for wrap in (False, True):
+            for rot in (False, True):
+                perm[(wrap, rot)] = const.tile([P, P], F32, name="perm%d%d" % (int(wrap), int(rot)))
+
+        def fill(eng, dst, src, rot):
+            if rot:
+                eng.tensor_copy(out=dst[:, :, 0:7, :], in_=src[:, :, 1:8, :])
+                eng.tensor_copy(out=dst[:, :, 7:8, :], in_=src[:, :, 0:1, :])
+            else:
+                eng.tensor_copy(out=dst, in_=src)
+
+        src_n = ident[:].rearrange("p (g tp e a) -> p e g a tp", g=2, tp=4, e=2)
+        src_w = ident[:].rearrange("p (tlh e a g th) -> p e g th a tlh", tlh=2, e=2, a=8, g=2)
+        for rot in (False, True):
+            dst_n = perm[(False, rot)][:].rearrange("p (e g a tp) -> p e g a tp", e=2, g=2, a=8)
+            for e in range(2):
+                fill(nc.gpsimd, dst_n[:, e], src_n[:, e], rot)
+        for rot in (False, True):
+            dst_w = perm[(True, rot)][:].rearrange("p (e g a th tlh) -> p e g th a tlh", e=2, g=2, a=8, th=2)
+            for e in range(2):
+                for g in range(2):
+                    fill(nc.vector, dst_w[:, e, g], src_w[:, e, g], rot)
 
         w_grp = const.tile([P, 3, P, 4], BF16, name="w_grp", align_bytes=64)
         w_codes = const.tile([P, 384], U32, name="w_codes", align_bytes=64)
@@ -111,110 +118,83 @@ def tile_windowattentionblock_pa_t_kernel(tc, x, wq, bq, wk, bk, wv, bv, out_0, 
             nc.tensor.matmul(out=bias_ps[:], lhsT=ones[:], rhs=b_row[:], start=True, stop=True)
             nc.scalar.copy(out=bias_sb[:].rearrange("p m f -> p (m f)"), in_=bias_ps[:, 0:384])
 
-        units = [(k, hb) for k in SLABS for hb in range(2)]
-        state = {}
+        grouped = {}
+        quantised = {}
+        o_tiles = {}
 
-        def transposes(h):
-            ti, hb = units[h]
-            if ti % 4 == 3:
-                perm = paw if hb == 0 else pbw
-            else:
-                perm = pa if hb == 0 else pb
-            xf = x_sb[ti][:].bitcast(F32)
+        def transposes(u):
+            grp, v = divmod(u, 4)
             g = gpool.tile([P, 2048], BF16, name="g", align_bytes=64)
-            gf = g[:].bitcast(F32).rearrange("p (a r u) -> p a r u", a=4, u=2)
-            for a2 in range(2):
+            gf = g[:].bitcast(F32).rearrange("p (t c w) -> p t c w", t=4, w=2)
+            for sl in range(2):
+                k = 2 * grp + sl
+                pm = perm[(k % 4 == 3, v >= 2)]
+                xf = x_sb[k][:].bitcast(F32)
                 xt = psum_t.tile([P, 2, 2, P], F32, name="xt")
-                for a in range(2):
-                    rj = (4 * hb + 2 * a2 + a + 4) % 8
-                    for u in range(2):
-                        c0 = rj * 256 + u * P
-                        nc.tensor.transpose(xt[:, a, u, :], xf[:, c0:c0 + P], perm[:])
-                nc.scalar.copy(out=gf[:, 2 * a2:2 * a2 + 2, :, :], in_=xt[:].rearrange("p a u r -> p a r u"))
-            state[("g", h)] = g
+                for i in range(2):
+                    rj = (2 * v + i + 4) % 8
+                    for w in range(2):
+                        c0 = rj * 256 + w * P
+                        nc.tensor.transpose(xt[:, w, i, :], xf[:, c0:c0 + P], pm[:])
+                nc.scalar.copy(
+                    out=gf[:, :, sl * 64:(sl + 1) * 64, :],
+                    in_=xt[:].rearrange("p w i (e c) -> p (i e) c w", e=2),
+                )
+            grouped[u] = g
 
-        def quantise(h):
-            g = state[("g", h)]
+        def quantise(u):
             codes = qpool.tile([P, 512], U32, name="codes", align_bytes=64)
             scales = qpool.tile([P, 512], U8, name="scales", align_bytes=64)
-            nc.vector.quantize_mx(out=codes[:].bitcast(FP8X4), scales=scales[:], in_=g[:])
-            state[("q", h)] = (codes, scales)
+            nc.vector.quantize_mx(out=codes[:].bitcast(FP8X4), scales=scales[:], in_=grouped[u][:])
+            quantised[u] = (codes, scales)
 
-        def mx(out, codes, scales, a, n0, n1):
-            cols = slice(a * P, (a + 1) * P)
-            nc.tensor.matmul_mx(
-                out=out,
-                lhsT=codes[:, cols].bitcast(FP8X4),
-                lhsT_scale=scales[:, cols],
-                rhs=w_codes[:, n0:n1].bitcast(FP8X4),
-                rhs_scale=w_scales[:, n0:n1],
-                start=True,
-                stop=True,
-            )
-
-        def project(h, half):
-            ti, hb = units[h]
-            codes, scales = state[("q", h)]
-            if hb == 0 and half == 0:
-                state[("o", ti)] = opool.tile([P, 3, 8, P], F32, name="o_sb")
-            o_sb = state[("o", ti)]
-            if half == 0:
-                state[("z", h)] = psum_o.tile([P, 4, P], F32, name="acc")
-            zb = state[("z", h)]
-            qk = psum_o.tile([P, 2, 2, P], F32, name="acc")
-            for i in range(2):
-                a = 2 * half + i
-                mx(qk[:, i, :, :].rearrange("p m f -> p (m f)"), codes, scales, a, 0, 256)
-                mx(zb[:, a, :], codes, scales, a, 256, 384)
-            t0 = 4 * hb + 2 * half
-            nc.vector.tensor_tensor(
-                out=o_sb[:, 0:2, t0:t0 + 2, :],
-                in0=qk[:].rearrange("p t m f -> p m t f"),
-                in1=bias_sb[:, 0:2, :].unsqueeze(2).to_broadcast([P, 2, 2, P]),
-                op=mybir.AluOpType.add,
-            )
-            if half == 1:
-                v_sb = o_sb[:, 2, 4 * hb:4 * hb + 4, :]
-                nc.scalar.copy(out=v_sb, in_=zb[:])
-                nc.gpsimd.tensor_tensor(
-                    out=v_sb,
-                    in0=v_sb,
-                    in1=bias_sb[:, 2:3, :].to_broadcast([P, 4, P]),
-                    op=mybir.AluOpType.add,
+        def job(j):
+            grp, jj = divmod(j, 12)
+            m, v = divmod(jj, 4)
+            codes, scales = quantised[4 * grp + v]
+            if v == 0:
+                o_tiles[(grp, m)] = opool.tile([P, 2, 8, P], F32, name="o_sb")
+            o_sb = o_tiles[(grp, m)]
+            acc = psum_o.tile([P, 4, P], F32, name="acc")
+            for t in range(4):
+                nc.tensor.matmul_mx(
+                    out=acc[:, t, :],
+                    lhsT=codes[:, t * P:(t + 1) * P].bitcast(FP8X4),
+                    lhsT_scale=scales[:, t * P:(t + 1) * P],
+                    rhs=w_codes[:, m * P:(m + 1) * P].bitcast(FP8X4),
+                    rhs_scale=w_scales[:, m * P:(m + 1) * P],
+                    start=True,
+                    stop=True,
                 )
-
-        def store(ti, t0, t1):
-            o_sb = state[("o", ti)]
-            for m in range(3):
+            dst = o_sb[:, :, 2 * v:2 * v + 2, :]
+            src = acc[:].rearrange("p (i e) f -> p e i f", e=2)
+            bias = bias_sb[:, m:m + 1, :].unsqueeze(1).to_broadcast([P, 2, 2, P])
+            if v == 0:
+                nc.scalar.copy(out=dst, in_=src)
+                nc.gpsimd.tensor_tensor(out=dst, in0=dst, in1=bias, op=ADD)
+            else:
+                nc.vector.tensor_tensor(out=dst, in0=src, in1=bias, op=ADD)
+            if v == 3:
                 nc.sync.dma_start(
-                    out=outs[m][ti * P:(ti + 1) * P, t0 * P:t1 * P],
-                    in_=o_sb[:, m, t0:t1, :].rearrange("p t f -> p (t f)"),
+                    out=outs[m][grp * P:(grp + 1) * P, :],
+                    in_=o_sb[:].rearrange("p e t f -> p (e t f)"),
                 )
 
-        n_units = len(units)
-        done = {"t": 0, "q": 0}
+        def job_of_transposes(u):
+            grp, v = divmod(u, 4)
+            return max(v - 1, 0) if grp == 0 else 12 * (grp - 1) + 4 + 2 * v
 
-        def transposes_upto(last):
-            while done["t"] <= min(last, n_units - 1):
-                transposes(done["t"])
-                done["t"] += 1
+        def job_of_quantise(u):
+            grp, v = divmod(u, 4)
+            return v if grp == 0 else 12 * (grp - 1) + 6 + 2 * v
 
-        def quantise_upto(last):
-            while done["q"] <= min(last, n_units - 1):
-                quantise(done["q"])
-                done["q"] += 1
-
-        transposes_upto(0)
-        quantise_upto(0)
-        for h in range(n_units):
-            ti, hb = units[h]
-            transposes_upto(h + min(LOOK_T, h + 1))
-            if h == 0:
+        for j in range(N_JOBS):
+            for u in range(N_UNITS):
+                if job_of_transposes(u) == j:
+                    transposes(u)
+            if j == 0:
                 spread_bias()
-            project(h, 0)
-            quantise_upto(h + min(LOOK_Q, h + 1))
-            project(h, 1)
-            if h >= n_units - 2:
-                store(ti, 4 * hb, 4 * hb + 4)
-            elif hb == 1:
-                store(ti, 0, 8)
+            for u in range(N_UNITS):
+                if job_of_quantise(u) == j:
+                    quantise(u)
+            job(j)

@@ -150,7 +150,10 @@ def tile_windowattentionblock_pa_t_kernel(tc, x, wq, bq, wk, bk, wv, bv, out_0, 
 
         def job(j):
             grp, jj = divmod(j, 12)
-            m, v = divmod(jj, 4)
+            if grp == 0:
+                v, m = divmod(jj, 3)
+            else:
+                m, v = divmod(jj, 4)
             codes, scales = quantised[4 * grp + v]
             if v == 0:
                 o_tiles[(grp, m)] = opool.tile([P, 2, 8, P], F32, name="o_sb")
@@ -169,7 +172,7 @@ def tile_windowattentionblock_pa_t_kernel(tc, x, wq, bq, wk, bk, wv, bv, out_0, 
             dst = o_sb[:, :, 2 * v:2 * v + 2, :]
             src = acc[:].rearrange("p (i e) f -> p e i f", e=2)
             bias = bias_sb[:, m:m + 1, :].unsqueeze(1).to_broadcast([P, 2, 2, P])
-            if v == 0:
+            if j % 3 == 0:
                 nc.scalar.copy(out=dst, in_=src)
                 nc.gpsimd.tensor_tensor(out=dst, in0=dst, in1=bias, op=ADD)
             else:
@@ -182,11 +185,19 @@ def tile_windowattentionblock_pa_t_kernel(tc, x, wq, bq, wk, bk, wv, bv, out_0, 
 
         def job_of_transposes(u):
             grp, v = divmod(u, 4)
-            return max(v - 1, 0) if grp == 0 else 12 * (grp - 1) + 4 + 2 * v
+            if grp == 0:
+                return max(v - 1, 0)
+            if grp == 1:
+                return 7 + v
+            return 12 * (grp - 1) + 4 + 2 * v
 
         def job_of_quantise(u):
             grp, v = divmod(u, 4)
-            return v if grp == 0 else 12 * (grp - 1) + 6 + 2 * v
+            if grp == 0:
+                return v
+            if grp == 1:
+                return 9 + v
+            return 12 * (grp - 1) + 6 + 2 * v
 
         for j in range(N_JOBS):
             for u in range(N_UNITS):

@@ -8,31 +8,32 @@ BF16 = mybir.dt.bfloat16
 F32 = mybir.dt.float32
 U32 = mybir.dt.uint32
 U8 = mybir.dt.uint8
-ADD = mybir.AluOpType.add
 
 P = 128
 FLOPS = 2 * 8192 * 512 * 384
-N_GROUPS = 4
-N_UNITS = 16
-N_JOBS = 48
+MANUAL = False
+LOOK_T = 3
+LOOK_Q = 2
+SLABS = (0, 1, 3, 2, 7, 4, 5, 6)
 
 
 def tile_windowattentionblock_pa_t_kernel(tc, x, wq, bq, wk, bk, wv, bv, out_0, out_1, out_2):
     nc = tc.nc
     weights = (wq, wk, wv)
     biases = (bq, bk, bv)
-    outs = [o.rearrange("n (tp r) h d -> (n tp) (r h d)", r=16) for o in (out_0, out_1, out_2)]
+    outs = [o.rearrange("n (ti tj) h d -> (n ti) (tj h d)", tj=8) for o in (out_0, out_1, out_2)]
     xc = x.rearrange("b i (aj rj) c -> (b i aj) (rj c)", rj=8)
 
     with ExitStack() as ctx:
         const = ctx.enter_context(tc.tile_pool(name="const", bufs=1))
         xpool = ctx.enter_context(tc.tile_pool(name="xpool", bufs=1))
         gpool = ctx.enter_context(tc.tile_pool(name="gpool", bufs=3))
-        qpool = ctx.enter_context(tc.tile_pool(name="qpool", bufs=8))
-        opool = ctx.enter_context(tc.tile_pool(name="opool", bufs=12))
+        qpool = ctx.enter_context(tc.tile_pool(name="qpool", bufs=4))
+        opool = ctx.enter_context(tc.tile_pool(name="opool", bufs=8))
         psum_t = ctx.enter_context(tc.psum_pool(name="psum_t", bufs=2))
         psum_o = ctx.enter_context(tc.psum_pool(name="psum_o", bufs=6))
-        ctx.enter_context(tc.manual_schedule())
+        if MANUAL:
+            ctx.enter_context(tc.manual_schedule())
 
         b_row = const.tile([P, 512], BF16, name="b_row")
         nc.vector.memset(b_row[:], 0.0)
@@ -45,55 +46,47 @@ def tile_windowattentionblock_pa_t_kernel(tc, x, wq, bq, wk, bk, wv, bv, out_0, 
                 out=w_raw[:, m, :, :].rearrange("p (u e) f -> p u (e f)", u=2),
                 in_=weights[m].rearrange("(u p e) h d -> p u (e h d)", u=2, e=2),
             )
-        x_sb = [xpool.tile([P, 4096], BF16, name="x%d" % k) for k in range(8)]
-
-        def first_chunk(k):
+        x_sb = {}
+        for pos, k in enumerate(SLABS):
+            x_t = xpool.tile([P, 4096], BF16, name="x%d" % k)
+            x_sb[k] = x_t
             b, a = divmod(k, 4)
-            return (b * 64 + 16 * a + 4) * 8
-
-        for lo in (2048, 0):
-            for k in range(2):
-                c0 = first_chunk(k)
-                nc.sync.dma_start(out=x_sb[k][:, lo:lo + 2048], in_=xc[c0:c0 + P, lo:lo + 2048])
-        for m in range(3):
-            nc.sync.dma_start(
-                out=b_row[0:1, m * P:(m + 1) * P],
-                in_=biases[m].rearrange("(o h) d -> o (h d)", o=1),
-            )
-        for k in range(2, 8):
-            c0 = first_chunk(k)
-            if k % 4 < 3:
-                nc.sync.dma_start(out=x_sb[k][:], in_=xc[c0:c0 + P, :])
+            c0 = (b * 64 + 16 * a + 4) * 8
+            if pos == 0:
+                nc.sync.dma_start(out=x_t[:, 2048:4096], in_=xc[c0:c0 + P, 2048:4096])
+                nc.sync.dma_start(out=x_t[:, 0:2048], in_=xc[c0:c0 + P, 0:2048])
+                for m in range(3):
+                    nc.sync.dma_start(
+                        out=b_row[0:1, m * P:(m + 1) * P],
+                        in_=biases[m].rearrange("(o h) d -> o (h d)", o=1),
+                    )
+            elif a < 3:
+                nc.sync.dma_start(out=x_t[:], in_=xc[c0:c0 + P, :])
             else:
                 for s in range(4):
-                    cs = c0 + 32 * s if s < 3 else (k // 4) * 512
-                    nc.sync.dma_start(out=x_sb[k][s:P:4, :], in_=xc[cs:cs + 32, :])
+                    cs = c0 + 32 * s if s < 3 else b * 512
+                    nc.sync.dma_start(out=x_t[s:P:4, :], in_=xc[cs:cs + 32, :])
+
 
         ident = const.tile([P, P], F32, name="ident")
         make_identity(nc, ident[:])
-        perm = {}
-        for wrap in (False, True):
-            for rot in (False, True):
-                perm[(wrap, rot)] = const.tile([P, P], F32, name="perm%d%d" % (int(wrap), int(rot)))
-
-        def fill(eng, dst, src, rot):
-            if rot:
-                eng.tensor_copy(out=dst[:, :, 0:7, :], in_=src[:, :, 1:8, :])
-                eng.tensor_copy(out=dst[:, :, 7:8, :], in_=src[:, :, 0:1, :])
-            else:
-                eng.tensor_copy(out=dst, in_=src)
-
-        src_n = ident[:].rearrange("p (g tp e a) -> p e g a tp", g=2, tp=4, e=2)
-        src_w = ident[:].rearrange("p (tlh e a g th) -> p e g th a tlh", tlh=2, e=2, a=8, g=2)
-        for rot in (False, True):
-            dst_n = perm[(False, rot)][:].rearrange("p (e g a tp) -> p e g a tp", e=2, g=2, a=8)
-            for e in range(2):
-                fill(nc.gpsimd, dst_n[:, e], src_n[:, e], rot)
-        for rot in (False, True):
-            dst_w = perm[(True, rot)][:].rearrange("p (e g a th tlh) -> p e g th a tlh", e=2, g=2, a=8, th=2)
-            for e in range(2):
-                for g in range(2):
-                    fill(nc.vector, dst_w[:, e, g], src_w[:, e, g], rot)
+        pa = const.tile([P, P], F32, name="pa")
+        pb = const.tile([P, P], F32, name="pb")
+        src = ident[:].rearrange("p (g t a) -> p g a t", g=2, t=8)
+        pav = pa[:].rearrange("p (g a t) -> p g a t", g=2, a=8)
+        pbv = pb[:].rearrange("p (g a t) -> p g a t", g=2, a=8)
+        nc.gpsimd.tensor_copy(out=pav, in_=src)
+        nc.gpsimd.tensor_copy(out=pbv[:, :, 0:7, :], in_=src[:, :, 1:8, :])
+        nc.gpsimd.tensor_copy(out=pbv[:, :, 7:8, :], in_=src[:, :, 0:1, :])
+        paw = const.tile([P, P], F32, name="paw")
+        pbw = const.tile([P, P], F32, name="pbw")
+        srcw = ident[:].rearrange("p (tl a g th) -> p g a th tl", tl=4, a=8, g=2)
+        pawv = paw[:].rearrange("p (g a th tl) -> p g a th tl", g=2, a=8, th=2)
+        pbwv = pbw[:].rearrange("p (g a th tl) -> p g a th tl", g=2, a=8, th=2)
+        for gg in range(2):
+            nc.vector.tensor_copy(out=pawv[:, gg, :, :, :], in_=srcw[:, gg, :, :, :])
+            nc.vector.tensor_copy(out=pbwv[:, gg, 0:7, :, :], in_=srcw[:, gg, 1:8, :, :])
+            nc.vector.tensor_copy(out=pbwv[:, gg, 7:8, :, :], in_=srcw[:, gg, 0:1, :, :])
 
         w_grp = const.tile([P, 3, P, 4], BF16, name="w_grp", align_bytes=64)
         w_codes = const.tile([P, 384], U32, name="w_codes", align_bytes=64)
@@ -118,94 +111,110 @@ def tile_windowattentionblock_pa_t_kernel(tc, x, wq, bq, wk, bk, wv, bv, out_0, 
             nc.tensor.matmul(out=bias_ps[:], lhsT=ones[:], rhs=b_row[:], start=True, stop=True)
             nc.scalar.copy(out=bias_sb[:].rearrange("p m f -> p (m f)"), in_=bias_ps[:, 0:384])
 
-        grouped = {}
-        quantised = {}
-        o_tiles = {}
+        units = [(k, hb) for k in SLABS for hb in range(2)]
+        state = {}
 
-        def transposes(u):
-            grp, v = divmod(u, 4)
+        def transposes(h):
+            ti, hb = units[h]
+            if ti % 4 == 3:
+                perm = paw if hb == 0 else pbw
+            else:
+                perm = pa if hb == 0 else pb
+            xf = x_sb[ti][:].bitcast(F32)
             g = gpool.tile([P, 2048], BF16, name="g", align_bytes=64)
-            gf = g[:].bitcast(F32).rearrange("p (t c w) -> p t c w", t=4, w=2)
-            for sl in range(2):
-                k = 2 * grp + sl
-                pm = perm[(k % 4 == 3, v >= 2)]
-                xf = x_sb[k][:].bitcast(F32)
+            gf = g[:].bitcast(F32).rearrange("p (a r u) -> p a r u", a=4, u=2)
+            for a2 in range(2):
                 xt = psum_t.tile([P, 2, 2, P], F32, name="xt")
-                for i in range(2):
-                    rj = (2 * v + i + 4) % 8
-                    for w in range(2):
-                        c0 = rj * 256 + w * P
-                        nc.tensor.transpose(xt[:, w, i, :], xf[:, c0:c0 + P], pm[:])
-                nc.scalar.copy(
-                    out=gf[:, :, sl * 64:(sl + 1) * 64, :],
-                    in_=xt[:].rearrange("p w i (e c) -> p (i e) c w", e=2),
-                )
-            grouped[u] = g
+                for a in range(2):
+                    rj = (4 * hb + 2 * a2 + a + 4) % 8
+                    for u in range(2):
+                        c0 = rj * 256 + u * P
+                        nc.tensor.transpose(xt[:, a, u, :], xf[:, c0:c0 + P], perm[:])
+                nc.scalar.copy(out=gf[:, 2 * a2:2 * a2 + 2, :, :], in_=xt[:].rearrange("p a u r -> p a r u"))
+            state[("g", h)] = g
 
-        def quantise(u):
+        def quantise(h):
+            g = state[("g", h)]
             codes = qpool.tile([P, 512], U32, name="codes", align_bytes=64)
             scales = qpool.tile([P, 512], U8, name="scales", align_bytes=64)
-            nc.vector.quantize_mx(out=codes[:].bitcast(FP8X4), scales=scales[:], in_=grouped[u][:])
-            quantised[u] = (codes, scales)
+            nc.vector.quantize_mx(out=codes[:].bitcast(FP8X4), scales=scales[:], in_=g[:])
+            state[("q", h)] = (codes, scales)
 
-        def job(j):
-            grp, jj = divmod(j, 12)
-            if grp == 0:
-                v, m = divmod(jj, 3)
-            else:
-                m, v = divmod(jj, 4)
-            codes, scales = quantised[4 * grp + v]
-            if v == 0:
-                o_tiles[(grp, m)] = opool.tile([P, 2, 8, P], F32, name="o_sb")
-            o_sb = o_tiles[(grp, m)]
-            acc = psum_o.tile([P, 4, P], F32, name="acc")
-            for t in range(4):
-                nc.tensor.matmul_mx(
-                    out=acc[:, t, :],
-                    lhsT=codes[:, t * P:(t + 1) * P].bitcast(FP8X4),
-                    lhsT_scale=scales[:, t * P:(t + 1) * P],
-                    rhs=w_codes[:, m * P:(m + 1) * P].bitcast(FP8X4),
-                    rhs_scale=w_scales[:, m * P:(m + 1) * P],
-                    start=True,
-                    stop=True,
+        def mx(out, codes, scales, a, n0, n1):
+            cols = slice(a * P, (a + 1) * P)
+            nc.tensor.matmul_mx(
+                out=out,
+                lhsT=codes[:, cols].bitcast(FP8X4),
+                lhsT_scale=scales[:, cols],
+                rhs=w_codes[:, n0:n1].bitcast(FP8X4),
+                rhs_scale=w_scales[:, n0:n1],
+                start=True,
+                stop=True,
+            )
+
+        def project(h, half):
+            ti, hb = units[h]
+            codes, scales = state[("q", h)]
+            if hb == 0 and half == 0:
+                state[("o", ti)] = opool.tile([P, 3, 8, P], F32, name="o_sb")
+            o_sb = state[("o", ti)]
+            if half == 0:
+                state[("z", h)] = psum_o.tile([P, 4, P], F32, name="acc")
+            zb = state[("z", h)]
+            qk = psum_o.tile([P, 2, 2, P], F32, name="acc")
+            for i in range(2):
+                a = 2 * half + i
+                mx(qk[:, i, :, :].rearrange("p m f -> p (m f)"), codes, scales, a, 0, 256)
+                mx(zb[:, a, :], codes, scales, a, 256, 384)
+            t0 = 4 * hb + 2 * half
+            nc.vector.tensor_tensor(
+                out=o_sb[:, 0:2, t0:t0 + 2, :],
+                in0=qk[:].rearrange("p t m f -> p m t f"),
+                in1=bias_sb[:, 0:2, :].unsqueeze(2).to_broadcast([P, 2, 2, P]),
+                op=mybir.AluOpType.add,
+            )
+            if half == 1:
+                v_sb = o_sb[:, 2, 4 * hb:4 * hb + 4, :]
+                nc.scalar.copy(out=v_sb, in_=zb[:])
+                nc.gpsimd.tensor_tensor(
+                    out=v_sb,
+                    in0=v_sb,
+                    in1=bias_sb[:, 2:3, :].to_broadcast([P, 4, P]),
+                    op=mybir.AluOpType.add,
                 )
-            dst = o_sb[:, :, 2 * v:2 * v + 2, :]
-            src = acc[:].rearrange("p (i e) f -> p e i f", e=2)
-            bias = bias_sb[:, m:m + 1, :].unsqueeze(1).to_broadcast([P, 2, 2, P])
-            if j % 3 == 0:
-                nc.scalar.copy(out=dst, in_=src)
-                nc.gpsimd.tensor_tensor(out=dst, in0=dst, in1=bias, op=ADD)
-            else:
-                nc.vector.tensor_tensor(out=dst, in0=src, in1=bias, op=ADD)
-            if v == 3:
+
+        def store(ti, t0, t1):
+            o_sb = state[("o", ti)]
+            for m in range(3):
                 nc.sync.dma_start(
-                    out=outs[m][grp * P:(grp + 1) * P, :],
-                    in_=o_sb[:].rearrange("p e t f -> p (e t f)"),
+                    out=outs[m][ti * P:(ti + 1) * P, t0 * P:t1 * P],
+                    in_=o_sb[:, m, t0:t1, :].rearrange("p t f -> p (t f)"),
                 )
 
-        def job_of_transposes(u):
-            grp, v = divmod(u, 4)
-            if grp == 0:
-                return max(v - 1, 0)
-            if grp == 1:
-                return 7 + v
-            return 12 * (grp - 1) + 4 + 2 * v
+        n_units = len(units)
+        done = {"t": 0, "q": 0}
 
-        def job_of_quantise(u):
-            grp, v = divmod(u, 4)
-            if grp == 0:
-                return v
-            if grp == 1:
-                return 9 + v
-            return 12 * (grp - 1) + 6 + 2 * v
+        def transposes_upto(last):
+            while done["t"] <= min(last, n_units - 1):
+                transposes(done["t"])
+                done["t"] += 1
 
-        for j in range(N_JOBS):
-            for u in range(N_UNITS):
-                if job_of_transposes(u) == j:
-                    transposes(u)
-            if j == 0:
+        def quantise_upto(last):
+            while done["q"] <= min(last, n_units - 1):
+                quantise(done["q"])
+                done["q"] += 1
+
+        transposes_upto(0)
+        quantise_upto(0)
+        for h in range(n_units):
+            ti, hb = units[h]
+            transposes_upto(h + min(LOOK_T, h + 1))
+            if h == 0:
                 spread_bias()
-            for u in range(N_UNITS):
-                if job_of_quantise(u) == j:
-                    quantise(u)
-            job(j)
+            project(h, 0)
+            quantise_upto(h + min(LOOK_Q, h + 1))
+            project(h, 1)
+            if h >= n_units - 2:
+                store(ti, 4 * hb, 4 * hb + 4)
+            elif hb == 1:
+                store(ti, 0, 8)

@@ -11,7 +11,7 @@ U8 = mybir.dt.uint8
 
 P = 128
 FLOPS = 2 * 8192 * 512 * 384
-MANUAL = False
+MANUAL = True
 LOOK_T = 3
 LOOK_Q = 2
 SLABS = (0, 1, 3, 2, 7, 4, 5, 6)
@@ -46,21 +46,18 @@ def tile_windowattentionblock_pa_t_kernel(tc, x, wq, bq, wk, bk, wv, bv, out_0, 
                 out=w_raw[:, m, :, :].rearrange("p (u e) f -> p u (e f)", u=2),
                 in_=weights[m].rearrange("(u p e) h d -> p u (e h d)", u=2, e=2),
             )
+        for m in range(3):
+            nc.scalar.dma_start(
+                out=b_row[0:1, m * P:(m + 1) * P],
+                in_=biases[m].rearrange("(o h) d -> o (h d)", o=1),
+            )
         x_sb = {}
         for pos, k in enumerate(SLABS):
             x_t = xpool.tile([P, 4096], BF16, name="x%d" % k)
             x_sb[k] = x_t
             b, a = divmod(k, 4)
             c0 = (b * 64 + 16 * a + 4) * 8
-            if pos == 0:
-                nc.sync.dma_start(out=x_t[:, 2048:4096], in_=xc[c0:c0 + P, 2048:4096])
-                nc.sync.dma_start(out=x_t[:, 0:2048], in_=xc[c0:c0 + P, 0:2048])
-                for m in range(3):
-                    nc.sync.dma_start(
-                        out=b_row[0:1, m * P:(m + 1) * P],
-                        in_=biases[m].rearrange("(o h) d -> o (h d)", o=1),
-                    )
-            elif a < 3:
+            if a < 3:
                 nc.sync.dma_start(out=x_t[:], in_=xc[c0:c0 + P, :])
             else:
                 for s in range(4):

from contextlib import ExitStack

import concourse.mybir as mybir
from concourse.masks import make_identity

FP8X4 = mybir.dt.float8_e4m3fn_x4
BF16 = mybir.dt.bfloat16
F32 = mybir.dt.float32
U32 = mybir.dt.uint32
U8 = mybir.dt.uint8

P = 128
FLOPS = 2 * 8192 * 512 * 384
MANUAL = True
LOOK_T = 3
LOOK_Q = 2
SLABS = (0, 1, 3, 2, 7, 4, 5, 6)


def tile_windowattentionblock_pa_t_kernel(tc, x, wq, bq, wk, bk, wv, bv, out_0, out_1, out_2):
    nc = tc.nc
    weights = (wq, wk, wv)
    biases = (bq, bk, bv)
    outs = [o.rearrange("n (ti tj) h d -> (n ti) (tj h d)", tj=8) for o in (out_0, out_1, out_2)]
    xc = x.rearrange("b i (aj rj) c -> (b i aj) (rj c)", rj=8)

    with ExitStack() as ctx:
        const = ctx.enter_context(tc.tile_pool(name="const", bufs=1))
        xpool = ctx.enter_context(tc.tile_pool(name="xpool", bufs=1))
        gpool = ctx.enter_context(tc.tile_pool(name="gpool", bufs=3))
        qpool = ctx.enter_context(tc.tile_pool(name="qpool", bufs=4))
        opool = ctx.enter_context(tc.tile_pool(name="opool", bufs=8))
        psum_t = ctx.enter_context(tc.psum_pool(name="psum_t", bufs=2))
        psum_o = ctx.enter_context(tc.psum_pool(name="psum_o", bufs=6))
        if MANUAL:
            ctx.enter_context(tc.manual_schedule())

        b_row = const.tile([P, 512], BF16, name="b_row")
        nc.vector.memset(b_row[:], 0.0)
        ones = const.tile([P, P], BF16, name="ones")
        nc.vector.memset(ones[:], 1.0)

        w_raw = const.tile([P, 3, 4, P], BF16, name="w_raw")
        for m in range(3):
            nc.scalar.dma_start(
                out=w_raw[:, m, :, :].rearrange("p (u e) f -> p u (e f)", u=2),
                in_=weights[m].rearrange("(u p e) h d -> p u (e h d)", u=2, e=2),
            )
        for m in range(3):
            nc.scalar.dma_start(
                out=b_row[0:1, m * P:(m + 1) * P],
                in_=biases[m].rearrange("(o h) d -> o (h d)", o=1),
            )
        x_sb = {}
        for pos, k in enumerate(SLABS):
            x_t = xpool.tile([P, 4096], BF16, name="x%d" % k)
            x_sb[k] = x_t
            b, a = divmod(k, 4)
            c0 = (b * 64 + 16 * a + 4) * 8
            if a < 3:
                nc.sync.dma_start(out=x_t[:], in_=xc[c0:c0 + P, :])
            else:
                for s in range(4):
                    cs = c0 + 32 * s if s < 3 else b * 512
                    nc.sync.dma_start(out=x_t[s:P:4, :], in_=xc[cs:cs + 32, :])


        ident = const.tile([P, P], F32, name="ident")
        make_identity(nc, ident[:])
        pa = const.tile([P, P], F32, name="pa")
        pb = const.tile([P, P], F32, name="pb")
        src = ident[:].rearrange("p (g t a) -> p g a t", g=2, t=8)
        pav = pa[:].rearrange("p (g a t) -> p g a t", g=2, a=8)
        pbv = pb[:].rearrange("p (g a t) -> p g a t", g=2, a=8)
        nc.gpsimd.tensor_copy(out=pav, in_=src)
        nc.gpsimd.tensor_copy(out=pbv[:, :, 0:7, :], in_=src[:, :, 1:8, :])
        nc.gpsimd.tensor_copy(out=pbv[:, :, 7:8, :], in_=src[:, :, 0:1, :])
        paw = const.tile([P, P], F32, name="paw")
        pbw = const.tile([P, P], F32, name="pbw")
        srcw = ident[:].rearrange("p (tl a g th) -> p g a th tl", tl=4, a=8, g=2)
        pawv = paw[:].rearrange("p (g a th tl) -> p g a th tl", g=2, a=8, th=2)
        pbwv = pbw[:].rearrange("p (g a th tl) -> p g a th tl", g=2, a=8, th=2)
        for gg in range(2):
            nc.vector.tensor_copy(out=pawv[:, gg, :, :, :], in_=srcw[:, gg, :, :, :])
            nc.vector.tensor_copy(out=pbwv[:, gg, 0:7, :, :], in_=srcw[:, gg, 1:8, :, :])
            nc.vector.tensor_copy(out=pbwv[:, gg, 7:8, :, :], in_=srcw[:, gg, 0:1, :, :])

        w_grp = const.tile([P, 3, P, 4], BF16, name="w_grp", align_bytes=64)
        w_codes = const.tile([P, 384], U32, name="w_codes", align_bytes=64)
        w_scales = const.tile([P, 384], U8, name="w_scales", align_bytes=64)
        for m in range(3):
            nc.vector.tensor_copy(out=w_grp[:, m, :, :], in_=w_raw[:, m, :, :].rearrange("p t f -> p f t"))
        nc.vector.quantize_mx(
            out=w_codes[:, 0:256].bitcast(FP8X4),
            scales=w_scales[:, 0:256],
            in_=w_grp[:, 0:2, :, :].rearrange("p m f t -> p (m f t)"),
        )
        nc.vector.quantize_mx(
            out=w_codes[:, 256:384].bitcast(FP8X4),
            scales=w_scales[:, 256:384],
            in_=w_grp[:, 2, :, :].rearrange("p f t -> p (f t)"),
        )

        bias_sb = const.tile([P, 3, P], F32, name="bias_sb")

        def spread_bias():
            bias_ps = psum_o.tile([P, 512], F32, name="acc")
            nc.tensor.matmul(out=bias_ps[:], lhsT=ones[:], rhs=b_row[:], start=True, stop=True)
            nc.scalar.copy(out=bias_sb[:].rearrange("p m f -> p (m f)"), in_=bias_ps[:, 0:384])

        units = [(k, hb) for k in SLABS for hb in range(2)]
        state = {}

        def transposes(h):
            ti, hb = units[h]
            if ti % 4 == 3:
                perm = paw if hb == 0 else pbw
            else:
                perm = pa if hb == 0 else pb
            xf = x_sb[ti][:].bitcast(F32)
            g = gpool.tile([P, 2048], BF16, name="g", align_bytes=64)
            gf = g[:].bitcast(F32).rearrange("p (a r u) -> p a r u", a=4, u=2)
            for a2 in range(2):
                xt = psum_t.tile([P, 2, 2, P], F32, name="xt")
                for a in range(2):
                    rj = (4 * hb + 2 * a2 + a + 4) % 8
                    for u in range(2):
                        c0 = rj * 256 + u * P
                        nc.tensor.transpose(xt[:, a, u, :], xf[:, c0:c0 + P], perm[:])
                nc.scalar.copy(out=gf[:, 2 * a2:2 * a2 + 2, :, :], in_=xt[:].rearrange("p a u r -> p a r u"))
            state[("g", h)] = g

        def quantise(h):
            g = state[("g", h)]
            codes = qpool.tile([P, 512], U32, name="codes", align_bytes=64)
            scales = qpool.tile([P, 512], U8, name="scales", align_bytes=64)
            nc.vector.quantize_mx(out=codes[:].bitcast(FP8X4), scales=scales[:], in_=g[:])
            state[("q", h)] = (codes, scales)

        def mx(out, codes, scales, a, n0, n1):
            cols = slice(a * P, (a + 1) * P)
            nc.tensor.matmul_mx(
                out=out,
                lhsT=codes[:, cols].bitcast(FP8X4),
                lhsT_scale=scales[:, cols],
                rhs=w_codes[:, n0:n1].bitcast(FP8X4),
                rhs_scale=w_scales[:, n0:n1],
                start=True,
                stop=True,
            )

        def project(h, half):
            ti, hb = units[h]
            codes, scales = state[("q", h)]
            if hb == 0 and half == 0:
                state[("o", ti)] = opool.tile([P, 3, 8, P], F32, name="o_sb")
            o_sb = state[("o", ti)]
            if half == 0:
                state[("z", h)] = psum_o.tile([P, 4, P], F32, name="acc")
            zb = state[("z", h)]
            qk = psum_o.tile([P, 2, 2, P], F32, name="acc")
            for i in range(2):
                a = 2 * half + i
                mx(qk[:, i, :, :].rearrange("p m f -> p (m f)"), codes, scales, a, 0, 256)
                mx(zb[:, a, :], codes, scales, a, 256, 384)
            t0 = 4 * hb + 2 * half
            nc.vector.tensor_tensor(
                out=o_sb[:, 0:2, t0:t0 + 2, :],
                in0=qk[:].rearrange("p t m f -> p m t f"),
                in1=bias_sb[:, 0:2, :].unsqueeze(2).to_broadcast([P, 2, 2, P]),
                op=mybir.AluOpType.add,
            )
            if half == 1:
                v_sb = o_sb[:, 2, 4 * hb:4 * hb + 4, :]
                nc.scalar.copy(out=v_sb, in_=zb[:])
                nc.gpsimd.tensor_tensor(
                    out=v_sb,
                    in0=v_sb,
                    in1=bias_sb[:, 2:3, :].to_broadcast([P, 4, P]),
                    op=mybir.AluOpType.add,
                )

        def store(ti, t0, t1):
            o_sb = state[("o", ti)]
            for m in range(3):
                nc.sync.dma_start(
                    out=outs[m][ti * P:(ti + 1) * P, t0 * P:t1 * P],
                    in_=o_sb[:, m, t0:t1, :].rearrange("p t f -> p (t f)"),
                )

        n_units = len(units)
        done = {"t": 0, "q": 0}

        def transposes_upto(last):
            while done["t"] <= min(last, n_units - 1):
                transposes(done["t"])
                done["t"] += 1

        def quantise_upto(last):
            while done["q"] <= min(last, n_units - 1):
                quantise(done["q"])
                done["q"] += 1

        transposes_upto(0)
        quantise_upto(0)
        for h in range(n_units):
            ti, hb = units[h]
            transposes_upto(h + min(LOOK_T, h + 1))
            if h == 0:
                spread_bias()
            project(h, 0)
            quantise_upto(h + min(LOOK_Q, h + 1))
            project(h, 1)
            if h >= n_units - 2:
                store(ti, 4 * hb, 4 * hb + 4)
            elif hb == 1:
                store(ti, 0, 8)
